import numpy as np
import ml_dtypes


def mxq(x, axis, fmt="e4m3"):
    dtype, down = {"e4m3": (ml_dtypes.float8_e4m3fn, 7), "e5m2": (ml_dtypes.float8_e5m2, 14)}[fmt]
    v = np.moveaxis(np.asarray(x, np.float32).astype(ml_dtypes.bfloat16).astype(np.float64), axis, -1)
    blocks = v.reshape(v.shape[:-1] + (-1, 32))
    amax = np.abs(blocks).max(-1, keepdims=True)
    byte = np.maximum(np.where(amax > 0, np.frexp(amax)[1] - 1 + 127, 0) - down, 1)
    scale = np.exp2(byte - 127.0)
    codes = (blocks / scale).astype(np.float32).astype(dtype).astype(np.float64)
    return np.moveaxis((codes * scale).reshape(v.shape), -1, axis)


WIDE = False


def mx_kscale(k):
    if not WIDE:
        return np.ones(k)
    levels = np.array([20, -20, 10, -10, 0])
    a = np.random.permutation(np.resize(levels, k // 512 * 4)).reshape(k // 512, 4)
    idx = np.arange(k)
    return np.exp2(a[idx // 512, idx % 128 // 32])


BF16 = ml_dtypes.bfloat16


def bf(x):
    return np.asarray(x, np.float32).astype(BF16)


def f64(x):
    return np.asarray(x).astype(np.float64)


B, C, H, W = 1, 512, 64, 64
OFFSETS = [(-1, 0), (1, 0), (0, -1), (0, 1), (-1, -1), (-1, 1), (1, -1), (1, 1)]


def _neighbor_mean(x):
    p = np.pad(x, ((0, 0), (0, 0), (1, 1), (1, 1)), mode="edge")
    h, w = x.shape[2], x.shape[3]
    s = None
    for dy, dx in OFFSETS:
        sl = p[:, :, 1 + dy:1 + dy + h, 1 + dx:1 + dx + w]
        s = sl if s is None else s + sl
    return s / 8.0


def _preact(x, Wp, b):
    n, c, h, w = x.shape
    mean = _neighbor_mean(x)
    z = Wp[:, :c] @ x.reshape(n, c, h * w) + Wp[:, c:] @ mean.reshape(n, c, h * w)
    return z.reshape(n, c, h, w) + b[None, :, None, None]


def setup_inputs():
    u = mx_kscale(C)
    u = u / u.max()
    x = bf(np.random.standard_normal((B, C, H, W)))
    Wp0 = bf(np.random.standard_normal((C, 2 * C)) / np.sqrt(C))
    b = bf(np.random.standard_normal(C) * 0.3)
    g = bf(np.random.standard_normal((B, C, H, W)) * np.exp2(np.random.randint(-12, 1, (B, 1, H, W))) * 8.0
           * u[None, :, None, None])
    z = _preact(f64(x), f64(Wp0), f64(b))
    return {"x": x, "Wp": bf(f64(Wp0) / u[:, None]), "b": b, "z": np.asarray(z, np.float32), "grad_out": g}


def reference(x, Wp, b, z, grad_out):
    g, Wf = f64(grad_out), f64(Wp)
    n, c, h, w = g.shape
    dz = g * (f64(z) > 0.0)
    dq = mxq(dz, 1, "e5m2").reshape(n, c, h * w)
    t = (mxq(Wf, 0, "e4m3").T @ dq).reshape(n, 2 * c, h, w)
    return g + t[:, :c] + _neighbor_mean(t[:, c:])

@@ -1,0 +1,153 @@
+import concourse.mybir as mybir
+
+F32 = mybir.dt.float32
+BF16 = mybir.dt.bfloat16
+U32 = mybir.dt.uint32
+U8 = mybir.dt.uint8
+E4M3X4 = mybir.dt.float8_e4m3fn_x4
+E5M2X4 = mybir.dt.float8_e5m2_x4
+ALU = mybir.AluOpType
+
+P = 128
+PACK = 4
+C = 512
+H = 64
+W = 64
+ROWS = 8
+N_TILE = ROWS * W
+BLOCKS = H // ROWS
+
+FLOPS = 2 * C * (2 * C) * H * W
+BYTES = 2 * C * (2 * C) + (4 + 2 + 4) * C * H * W
+
+
+def tile_staticgraphmodule_t_v_kernel(tc, x, Wp, b, z, grad_out, out):
+    nc = tc.nc
+    z_rows = z.rearrange("n (p t) h w -> (n p) t (h w)", t=PACK)
+    g_rows = grad_out.rearrange("n (p t) h w -> (n p) t (h w)", t=PACK)
+    out_rows = out.rearrange("n (p t) h w -> (n p) t (h w)", t=PACK)
+    w_rows = Wp.rearrange("(p t) m -> p t m", t=PACK)
+
+    with (
+        tc.tile_pool(name="keep", bufs=1) as keep,
+        tc.tile_pool(name="work", bufs=3) as work,
+        tc.tile_pool(name="result", bufs=4) as result,
+        tc.psum_pool(name="psum", bufs=4) as psum,
+    ):
+        w_raw = keep.tile([P, PACK, 2 * C], BF16)
+        nc.sync.dma_start(out=w_raw[:], in_=w_rows)
+        z_sb = keep.tile([P, PACK, H * W], F32)
+        g_sb = keep.tile([P, PACK, H * W], BF16)
+        for c in range(BLOCKS):
+            first = 0 if c == 0 else ROWS * c + 1
+            last = min(ROWS * c + ROWS, H - 1)
+            cols = slice(W * first, W * (last + 1))
+            nc.sync.dma_start(out=z_sb[:, :, cols], in_=z_rows[:, :, cols])
+            nc.sync.dma_start(out=g_sb[:, :, cols], in_=g_rows[:, :, cols])
+
+        w_grouped = keep.tile([P, 2 * C, PACK], BF16, align_bytes=64)
+        w_codes = keep.tile([P, 2 * C], U32, align_bytes=64)
+        w_scales = keep.tile([P, 2 * C], U8, align_bytes=64)
+        nc.vector.tensor_copy(
+            out=w_grouped[:, 0:C, :].rearrange("p (o q) t -> p o q t", o=PACK),
+            in_=w_raw[:, :, 0:C].rearrange("p t (q o) -> p o q t", o=PACK),
+        )
+        nc.scalar.mul(
+            out=w_grouped[:, C : 2 * C, :].rearrange("p (o q) t -> p o q t", o=PACK),
+            in_=w_raw[:, :, C : 2 * C].rearrange("p t (q o) -> p o q t", o=PACK),
+            mul=0.125,
+        )
+        for half in range(2):
+            m = slice(C * half, C * (half + 1))
+            nc.vector.quantize_mx(
+                out=w_codes[:, m].bitcast(E4M3X4),
+                scales=w_scales[:, m],
+                in_=w_grouped[:, m, :].rearrange("p m t -> p (m t)"),
+            )
+
+        dq_codes = keep.tile([P, (H + 2) * W], U32, align_bytes=64)
+        dq_scales = keep.tile([P, (H + 2) * W], U8, align_bytes=64)
+
+        def masked_gradient(dz, at, row, n_rows):
+            cols = slice(W * row, W * (row + n_rows))
+            nc.vector.scalar_tensor_tensor(
+                out=dz[:, W * at : W * (at + n_rows), :],
+                in0=z_sb[:, :, cols].rearrange("p t w -> p w t"),
+                scalar=0.0,
+                in1=g_sb[:, :, cols].rearrange("p t w -> p w t"),
+                op0=ALU.is_gt,
+                op1=ALU.mult,
+            )
+
+        def quantise(dz, padded_row, n_rows):
+            cols = slice(W * padded_row, W * (padded_row + n_rows))
+            nc.vector.quantize_mx(
+                out=dq_codes[:, cols].bitcast(E5M2X4),
+                scales=dq_scales[:, cols],
+                in_=dz[:, 0 : W * n_rows, :].rearrange("p w t -> p (w t)"),
+            )
+
+        def multiply(acc, half, o, block, dy, start, stop):
+            m = slice(C * half + P * o, C * half + P * (o + 1))
+            first = W * (ROWS * block + 1 + dy)
+            nc.tensor.matmul_mx(
+                out=acc[:],
+                lhsT=w_codes[:, m].bitcast(E4M3X4),
+                lhsT_scale=w_scales[:, m],
+                rhs=dq_codes[:, first : first + N_TILE].bitcast(E5M2X4),
+                rhs_scale=dq_scales[:, first : first + N_TILE],
+                start=start,
+                stop=stop,
+            )
+
+        dz = work.tile([P, N_TILE, PACK], BF16, align_bytes=64)
+        masked_gradient(dz, 0, 0, 1)
+        masked_gradient(dz, 1, 0, 1)
+        quantise(dz, 0, 2)
+
+        for block in range(BLOCKS):
+            dz = work.tile([P, N_TILE, PACK], BF16, align_bytes=64)
+            first = ROWS * block + 1
+            n_rows = min(ROWS, H - first)
+            masked_gradient(dz, 0, first, n_rows)
+            if n_rows < ROWS:
+                masked_gradient(dz, n_rows, H - 1, 1)
+            quantise(dz, ROWS * block + 2, ROWS)
+
+            cols = slice(N_TILE * block, N_TILE * (block + 1))
+            total = result.tile([P, PACK, ROWS, W], F32)
+            shifted = work.tile([P, PACK, ROWS, W + 1], F32)
+            for o in range(PACK):
+                vert = psum.tile([P, N_TILE], F32)
+                multiply(vert, 1, o, block, -1, True, False)
+                multiply(vert, 1, o, block, 0, False, False)
+                multiply(vert, 1, o, block, 1, False, True)
+                mid = psum.tile([P, N_TILE], F32)
+                multiply(mid, 1, o, block, -1, True, False)
+                multiply(mid, 1, o, block, 1, False, False)
+                multiply(mid, 0, o, block, 0, False, True)
+                vert_rows = vert[:].rearrange("p (r j) -> p r j", j=W)
+                nc.scalar.copy(out=shifted[:, o, :, 1 : W + 1], in_=vert_rows)
+                nc.scalar.copy(out=shifted[:, o, :, 0:1], in_=vert_rows[:, :, 0:1])
+                nc.vector.tensor_tensor(
+                    out=total[:, o, :, :].rearrange("p r j -> p (r j)"),
+                    in0=mid[:],
+                    in1=g_sb[:, o, cols],
+                    op=ALU.add,
+                )
+                nc.gpsimd.tensor_tensor(
+                    out=total[:, o, :, :], in0=total[:, o, :, :], in1=shifted[:, o, :, 0:W], op=ALU.add
+                )
+                nc.vector.tensor_tensor(
+                    out=total[:, o, :, 0 : W - 1],
+                    in0=total[:, o, :, 0 : W - 1],
+                    in1=vert_rows[:, :, 1:W],
+                    op=ALU.add,
+                )
+            nc.vector.tensor_tensor(
+                out=total[:, :, :, W - 1 : W],
+                in0=total[:, :, :, W - 1 : W],
+                in1=shifted[:, :, :, W : W + 1],
+                op=ALU.add,
+            )
+            nc.sync.dma_start(out=out_rows[:, :, cols], in_=total[:].rearrange("p o r j -> p o (r j)"))

@@ -16,6 +16,11 @@ W = 64
 ROWS = 8
 N_TILE = ROWS * W
 BLOCKS = H // ROWS
+TILES = BLOCKS * PACK
+PIECE_ROWS = 2
+PIECES = (H + 2) // PIECE_ROWS
+LEAD = 8
+RIGHT_LAG = 2
 
 FLOPS = 2 * C * (2 * C) * H * W
 BYTES = 2 * C * (2 * C) + (4 + 2 + 4) * C * H * W
@@ -33,14 +38,15 @@ def tile_staticgraphmodule_t_v_kernel(tc, x, Wp, b, z, grad_out, out):
         tc.tile_pool(name="work", bufs=3) as work,
         tc.tile_pool(name="result", bufs=4) as result,
         tc.psum_pool(name="psum", bufs=4) as psum,
+        tc.manual_schedule(),
     ):
         w_raw = keep.tile([P, PACK, 2 * C], BF16)
         nc.sync.dma_start(out=w_raw[:], in_=w_rows)
         z_sb = keep.tile([P, PACK, H * W], F32)
         g_sb = keep.tile([P, PACK, H * W], BF16)
-        for c in range(BLOCKS):
-            first = 0 if c == 0 else ROWS * c + 1
-            last = min(ROWS * c + ROWS, H - 1)
+        for block in range(BLOCKS):
+            first = 0 if block == 0 else ROWS * block + 1
+            last = min(ROWS * block + ROWS, H - 1)
             cols = slice(W * first, W * (last + 1))
             nc.sync.dma_start(out=z_sb[:, :, cols], in_=z_rows[:, :, cols])
             nc.sync.dma_start(out=g_sb[:, :, cols], in_=g_rows[:, :, cols])
@@ -67,6 +73,11 @@ def tile_staticgraphmodule_t_v_kernel(tc, x, Wp, b, z, grad_out, out):
 
         dq_codes = keep.tile([P, (H + 2) * W], U32, align_bytes=64)
         dq_scales = keep.tile([P, (H + 2) * W], U8, align_bytes=64)
+        masked = {}
+        verts = {}
+        mids = {}
+        totals = {}
+        shifteds = {}
 
         def masked_gradient(dz, at, row, n_rows):
             cols = slice(W * row, W * (row + n_rows))
@@ -79,19 +90,30 @@ def tile_staticgraphmodule_t_v_kernel(tc, x, Wp, b, z, grad_out, out):
                 op1=ALU.mult,
             )
 
-        def quantise(dz, padded_row, n_rows):
-            cols = slice(W * padded_row, W * (padded_row + n_rows))
+        def mask(piece):
+            dz = work.tile([P, PIECE_ROWS * W, PACK], BF16, align_bytes=64)
+            masked[piece] = dz
+            upper = min(max(PIECE_ROWS * piece - 1, 0), H - 1)
+            lower = min(PIECE_ROWS * piece, H - 1)
+            if lower == upper + 1:
+                masked_gradient(dz, 0, upper, 2)
+            else:
+                masked_gradient(dz, 0, upper, 1)
+                masked_gradient(dz, 1, lower, 1)
+
+        def quantise(piece):
+            cols = slice(PIECE_ROWS * W * piece, PIECE_ROWS * W * (piece + 1))
             nc.vector.quantize_mx(
                 out=dq_codes[:, cols].bitcast(E5M2X4),
                 scales=dq_scales[:, cols],
-                in_=dz[:, 0 : W * n_rows, :].rearrange("p w t -> p (w t)"),
+                in_=masked[piece][:].rearrange("p w t -> p (w t)"),
             )
 
         def multiply(acc, half, o, block, dy, start, stop):
             m = slice(C * half + P * o, C * half + P * (o + 1))
             first = W * (ROWS * block + 1 + dy)
             nc.tensor.matmul_mx(
-                out=acc[:],
+                out=acc[:].rearrange("p r j -> p (r j)"),
                 lhsT=w_codes[:, m].bitcast(E4M3X4),
                 lhsT_scale=w_scales[:, m],
                 rhs=dq_codes[:, first : first + N_TILE].bitcast(E5M2X4),
@@ -100,54 +122,69 @@ def tile_staticgraphmodule_t_v_kernel(tc, x, Wp, b, z, grad_out, out):
                 stop=stop,
             )
 
-        dz = work.tile([P, N_TILE, PACK], BF16, align_bytes=64)
-        masked_gradient(dz, 0, 0, 1)
-        masked_gradient(dz, 1, 0, 1)
-        quantise(dz, 0, 2)
+        def products(n):
+            block, o = divmod(n, PACK)
+            vert = psum.tile([P, ROWS, W], F32, bufs=5)
+            multiply(vert, 1, o, block, -1, True, False)
+            multiply(vert, 1, o, block, 0, False, False)
+            multiply(vert, 1, o, block, 1, False, True)
+            mid = psum.tile([P, ROWS, W], F32, bufs=3)
+            multiply(mid, 1, o, block, -1, True, False)
+            multiply(mid, 1, o, block, 1, False, False)
+            multiply(mid, 0, o, block, 0, False, True)
+            verts[n] = vert
+            mids[n] = mid
 
-        for block in range(BLOCKS):
-            dz = work.tile([P, N_TILE, PACK], BF16, align_bytes=64)
-            first = ROWS * block + 1
-            n_rows = min(ROWS, H - first)
-            masked_gradient(dz, 0, first, n_rows)
-            if n_rows < ROWS:
-                masked_gradient(dz, n_rows, H - 1, 1)
-            quantise(dz, ROWS * block + 2, ROWS)
-
-            cols = slice(N_TILE * block, N_TILE * (block + 1))
-            total = result.tile([P, PACK, ROWS, W], F32)
-            shifted = work.tile([P, PACK, ROWS, W + 1], F32)
-            for o in range(PACK):
-                vert = psum.tile([P, N_TILE], F32)
-                multiply(vert, 1, o, block, -1, True, False)
-                multiply(vert, 1, o, block, 0, False, False)
-                multiply(vert, 1, o, block, 1, False, True)
-                mid = psum.tile([P, N_TILE], F32)
-                multiply(mid, 1, o, block, -1, True, False)
-                multiply(mid, 1, o, block, 1, False, False)
-                multiply(mid, 0, o, block, 0, False, True)
-                vert_rows = vert[:].rearrange("p (r j) -> p r j", j=W)
-                nc.scalar.copy(out=shifted[:, o, :, 1 : W + 1], in_=vert_rows)
-                nc.scalar.copy(out=shifted[:, o, :, 0:1], in_=vert_rows[:, :, 0:1])
-                nc.vector.tensor_tensor(
-                    out=total[:, o, :, :].rearrange("p r j -> p (r j)"),
-                    in0=mid[:],
-                    in1=g_sb[:, o, cols],
-                    op=ALU.add,
-                )
-                nc.gpsimd.tensor_tensor(
-                    out=total[:, o, :, :], in0=total[:, o, :, :], in1=shifted[:, o, :, 0:W], op=ALU.add
-                )
-                nc.vector.tensor_tensor(
-                    out=total[:, o, :, 0 : W - 1],
-                    in0=total[:, o, :, 0 : W - 1],
-                    in1=vert_rows[:, :, 1:W],
-                    op=ALU.add,
-                )
+        def start_tile(n):
+            block, o = divmod(n, PACK)
+            if o == 0:
+                total = result.tile([P, PACK, ROWS, W], F32)
+                shifted = work.tile([P, PACK, ROWS, W + 1], F32)
+                totals[block] = total
+                shifteds[block] = shifted
+            nc.scalar.copy(out=shifteds[block][:, o, :, 1 : W + 1], in_=verts[n][:])
+            nc.scalar.copy(out=shifteds[block][:, o, :, 0:1], in_=verts[n][:, :, 0:1])
             nc.vector.tensor_tensor(
-                out=total[:, :, :, W - 1 : W],
-                in0=total[:, :, :, W - 1 : W],
-                in1=shifted[:, :, :, W : W + 1],
+                out=totals[block][:, o, :, :],
+                in0=mids[n][:],
+                in1=g_sb[:, o, N_TILE * block : N_TILE * (block + 1)].rearrange("p (r j) -> p r j", j=W),
                 op=ALU.add,
             )
-            nc.sync.dma_start(out=out_rows[:, :, cols], in_=total[:].rearrange("p o r j -> p o (r j)"))
+            nc.gpsimd.tensor_tensor(
+                out=totals[block][:, o, :, :],
+                in0=totals[block][:, o, :, :],
+                in1=shifteds[block][:, o, :, 0:W],
+                op=ALU.add,
+            )
+
+        def finish_tile(n):
+            block, o = divmod(n, PACK)
+            total = totals[block]
+            nc.vector.tensor_tensor(
+                out=total[:, o, :, 0 : W - 1],
+                in0=total[:, o, :, 0 : W - 1],
+                in1=verts[n][:, :, 1:W],
+                op=ALU.add,
+            )
+            if o == PACK - 1:
+                nc.vector.tensor_tensor(
+                    out=total[:, :, :, W - 1 : W],
+                    in0=total[:, :, :, W - 1 : W],
+                    in1=shifteds[block][:, :, :, W : W + 1],
+                    op=ALU.add,
+                )
+                nc.sync.dma_start(
+                    out=out_rows[:, :, N_TILE * block : N_TILE * (block + 1)],
+                    in_=total[:].rearrange("p o r j -> p o (r j)"),
+                )
+
+        for n in range(-LEAD, TILES + RIGHT_LAG):
+            if 0 <= n < TILES:
+                products(n)
+                start_tile(n)
+            if n + LEAD < PIECES:
+                mask(n + LEAD)
+            if 0 <= n - RIGHT_LAG:
+                finish_tile(n - RIGHT_LAG)
+            if 0 <= n + LEAD - 1 < PIECES:
+                quantise(n + LEAD - 1)

@@ -19,7 +19,7 @@ BLOCKS = H // ROWS
 TILES = BLOCKS * PACK
 PIECE_ROWS = 2
 PIECES = (H + 2) // PIECE_ROWS
-LEAD = 8
+LEAD = 9
 RIGHT_LAG = 2
 
 FLOPS = 2 * C * (2 * C) * H * W
@@ -79,27 +79,29 @@ def tile_staticgraphmodule_t_v_kernel(tc, x, Wp, b, z, grad_out, out):
         totals = {}
         shifteds = {}
 
-        def masked_gradient(dz, at, row, n_rows):
+        def masked_gradient(dz_rows, at, row, n_rows):
             cols = slice(W * row, W * (row + n_rows))
             nc.vector.scalar_tensor_tensor(
-                out=dz[:, W * at : W * (at + n_rows), :],
-                in0=z_sb[:, :, cols].rearrange("p t w -> p w t"),
+                out=dz_rows[:, :, W * at : W * (at + n_rows)],
+                in0=z_sb[:, :, cols],
                 scalar=0.0,
-                in1=g_sb[:, :, cols].rearrange("p t w -> p w t"),
+                in1=g_sb[:, :, cols],
                 op0=ALU.is_gt,
                 op1=ALU.mult,
             )
 
         def mask(piece):
-            dz = work.tile([P, PIECE_ROWS * W, PACK], BF16, align_bytes=64)
-            masked[piece] = dz
+            dz_rows = work.tile([P, PACK, PIECE_ROWS * W], BF16)
             upper = min(max(PIECE_ROWS * piece - 1, 0), H - 1)
             lower = min(PIECE_ROWS * piece, H - 1)
             if lower == upper + 1:
-                masked_gradient(dz, 0, upper, 2)
+                masked_gradient(dz_rows, 0, upper, 2)
             else:
-                masked_gradient(dz, 0, upper, 1)
-                masked_gradient(dz, 1, lower, 1)
+                masked_gradient(dz_rows, 0, upper, 1)
+                masked_gradient(dz_rows, 1, lower, 1)
+            dz = work.tile([P, PIECE_ROWS * W, PACK], BF16, align_bytes=64, bufs=4)
+            masked[piece] = dz
+            nc.scalar.copy(out=dz[:], in_=dz_rows[:].rearrange("p t w -> p w t"))
 
         def quantise(piece):
             cols = slice(PIECE_ROWS * W * piece, PIECE_ROWS * W * (piece + 1))
@@ -186,5 +188,5 @@ def tile_staticgraphmodule_t_v_kernel(tc, x, Wp, b, z, grad_out, out):
                 mask(n + LEAD)
             if 0 <= n - RIGHT_LAG:
                 finish_tile(n - RIGHT_LAG)
-            if 0 <= n + LEAD - 1 < PIECES:
-                quantise(n + LEAD - 1)
+            if 0 <= n + LEAD - 2 < PIECES:
+                quantise(n + LEAD - 2)

@@ -21,6 +21,8 @@ PIECE_ROWS = 2
 PIECES = (H + 2) // PIECE_ROWS
 LEAD = 9
 RIGHT_LAG = 2
+LEFT_LAG = 1
+GPSIMD_TILES = 3
 
 FLOPS = 2 * C * (2 * C) * H * W
 BYTES = 2 * C * (2 * C) + (4 + 2 + 4) * C * H * W
@@ -152,12 +154,23 @@ def tile_staticgraphmodule_t_v_kernel(tc, x, Wp, b, z, grad_out, out):
                 in1=g_sb[:, o, N_TILE * block : N_TILE * (block + 1)].rearrange("p (r j) -> p r j", j=W),
                 op=ALU.add,
             )
-            nc.gpsimd.tensor_tensor(
-                out=totals[block][:, o, :, :],
-                in0=totals[block][:, o, :, :],
-                in1=shifteds[block][:, o, :, 0:W],
-                op=ALU.add,
-            )
+            if o < GPSIMD_TILES:
+                nc.gpsimd.tensor_tensor(
+                    out=totals[block][:, o, :, :],
+                    in0=totals[block][:, o, :, :],
+                    in1=shifteds[block][:, o, :, 0:W],
+                    op=ALU.add,
+                )
+
+        def add_left_on_vector(n):
+            block, o = divmod(n, PACK)
+            if o >= GPSIMD_TILES:
+                nc.vector.tensor_tensor(
+                    out=totals[block][:, o, :, 1:W],
+                    in0=totals[block][:, o, :, 1:W],
+                    in1=verts[n][:, :, 0 : W - 1],
+                    op=ALU.add,
+                )
 
         def finish_tile(n):
             block, o = divmod(n, PACK)
@@ -169,6 +182,12 @@ def tile_staticgraphmodule_t_v_kernel(tc, x, Wp, b, z, grad_out, out):
                 op=ALU.add,
             )
             if o == PACK - 1:
+                nc.vector.tensor_tensor(
+                    out=total[:, GPSIMD_TILES:PACK, :, 0:1],
+                    in0=total[:, GPSIMD_TILES:PACK, :, 0:1],
+                    in1=shifteds[block][:, GPSIMD_TILES:PACK, :, 0:1],
+                    op=ALU.add,
+                )
                 nc.vector.tensor_tensor(
                     out=total[:, :, :, W - 1 : W],
                     in0=total[:, :, :, W - 1 : W],
@@ -186,6 +205,8 @@ def tile_staticgraphmodule_t_v_kernel(tc, x, Wp, b, z, grad_out, out):
                 start_tile(n)
             if n + LEAD < PIECES:
                 mask(n + LEAD)
+            if 0 <= n - LEFT_LAG < TILES:
+                add_left_on_vector(n - LEFT_LAG)
             if 0 <= n - RIGHT_LAG:
                 finish_tile(n - RIGHT_LAG)
             if 0 <= n + LEAD - 2 < PIECES:

@@ -17,9 +17,10 @@ ROWS = 8
 N_TILE = ROWS * W
 BLOCKS = H // ROWS
 TILES = BLOCKS * PACK
-PIECE_ROWS = 2
-PIECES = (H + 2) // PIECE_ROWS
-LEAD = 9
+PIECE_ROWS = 4
+PIECES = H // PIECE_ROWS + 1
+STEPS_A_PIECE = 2
+LEAD = 5
 RIGHT_LAG = 2
 LEFT_LAG = 1
 GPSIMD_TILES = 3
@@ -46,9 +47,9 @@ def tile_staticgraphmodule_t_v_kernel(tc, x, Wp, b, z, grad_out, out):
         nc.sync.dma_start(out=w_raw[:], in_=w_rows)
         z_sb = keep.tile([P, PACK, H * W], F32)
         g_sb = keep.tile([P, PACK, H * W], BF16)
-        for block in range(BLOCKS):
-            first = 0 if block == 0 else ROWS * block + 1
-            last = min(ROWS * block + ROWS, H - 1)
+        for piece in range(PIECES):
+            first = max(PIECE_ROWS * piece - 3, 0)
+            last = min(PIECE_ROWS * piece, H - 1)
             cols = slice(W * first, W * (last + 1))
             nc.sync.dma_start(out=z_sb[:, :, cols], in_=z_rows[:, :, cols])
             nc.sync.dma_start(out=g_sb[:, :, cols], in_=g_rows[:, :, cols])
@@ -81,6 +82,9 @@ def tile_staticgraphmodule_t_v_kernel(tc, x, Wp, b, z, grad_out, out):
         totals = {}
         shifteds = {}
 
+        def padded_rows(piece):
+            return max(PIECE_ROWS * piece - 2, 0), PIECE_ROWS * piece + 2
+
         def masked_gradient(dz_rows, at, row, n_rows):
             cols = slice(W * row, W * (row + n_rows))
             nc.vector.scalar_tensor_tensor(
@@ -93,24 +97,27 @@ def tile_staticgraphmodule_t_v_kernel(tc, x, Wp, b, z, grad_out, out):
             )
 
         def mask(piece):
+            rows = [min(max(r - 1, 0), H - 1) for r in range(*padded_rows(piece))]
             dz_rows = work.tile([P, PACK, PIECE_ROWS * W], BF16)
-            upper = min(max(PIECE_ROWS * piece - 1, 0), H - 1)
-            lower = min(PIECE_ROWS * piece, H - 1)
-            if lower == upper + 1:
-                masked_gradient(dz_rows, 0, upper, 2)
-            else:
-                masked_gradient(dz_rows, 0, upper, 1)
-                masked_gradient(dz_rows, 1, lower, 1)
-            dz = work.tile([P, PIECE_ROWS * W, PACK], BF16, align_bytes=64, bufs=4)
+            at = 0
+            while at < len(rows):
+                n_rows = 1
+                while at + n_rows < len(rows) and rows[at + n_rows] == rows[at] + n_rows:
+                    n_rows += 1
+                masked_gradient(dz_rows, at, rows[at], n_rows)
+                at += n_rows
+            dz = work.tile([P, PIECE_ROWS * W, PACK], BF16, align_bytes=64)
             masked[piece] = dz
-            nc.scalar.copy(out=dz[:], in_=dz_rows[:].rearrange("p t w -> p w t"))
+            width = W * len(rows)
+            nc.scalar.copy(out=dz[:, 0:width, :], in_=dz_rows[:, :, 0:width].rearrange("p t w -> p w t"))
 
         def quantise(piece):
-            cols = slice(PIECE_ROWS * W * piece, PIECE_ROWS * W * (piece + 1))
+            first, end = padded_rows(piece)
+            cols = slice(W * first, W * end)
             nc.vector.quantize_mx(
                 out=dq_codes[:, cols].bitcast(E5M2X4),
                 scales=dq_scales[:, cols],
-                in_=masked[piece][:].rearrange("p w t -> p (w t)"),
+                in_=masked[piece][:, 0 : W * (end - first), :].rearrange("p w t -> p (w t)"),
             )
 
         def multiply(acc, half, o, block, dy, start, stop):
@@ -199,15 +206,17 @@ def tile_staticgraphmodule_t_v_kernel(tc, x, Wp, b, z, grad_out, out):
                     in_=total[:].rearrange("p o r j -> p o (r j)"),
                 )
 
-        for n in range(-LEAD, TILES + RIGHT_LAG):
+        for n in range(-STEPS_A_PIECE * LEAD, TILES + RIGHT_LAG):
+            piece, phase = divmod(n, STEPS_A_PIECE)
+            piece += LEAD
             if 0 <= n < TILES:
                 products(n)
                 start_tile(n)
-            if n + LEAD < PIECES:
-                mask(n + LEAD)
+            if phase == 0 and piece < PIECES:
+                mask(piece)
             if 0 <= n - LEFT_LAG < TILES:
                 add_left_on_vector(n - LEFT_LAG)
             if 0 <= n - RIGHT_LAG:
                 finish_tile(n - RIGHT_LAG)
-            if 0 <= n + LEAD - 2 < PIECES:
-                quantise(n + LEAD - 2)
+            if phase == 0 and 0 <= piece - 1 < PIECES:
+                quantise(piece - 1)

@@ -47,9 +47,9 @@ def tile_staticgraphmodule_t_v_kernel(tc, x, Wp, b, z, grad_out, out):
         nc.sync.dma_start(out=w_raw[:], in_=w_rows)
         z_sb = keep.tile([P, PACK, H * W], F32)
         g_sb = keep.tile([P, PACK, H * W], BF16)
-        for piece in range(PIECES):
-            first = max(PIECE_ROWS * piece - 3, 0)
-            last = min(PIECE_ROWS * piece, H - 1)
+        for block in range(BLOCKS):
+            first = 0 if block == 0 else ROWS * block + 1
+            last = min(ROWS * block + ROWS, H - 1)
             cols = slice(W * first, W * (last + 1))
             nc.sync.dma_start(out=z_sb[:, :, cols], in_=z_rows[:, :, cols])
             nc.sync.dma_start(out=g_sb[:, :, cols], in_=g_rows[:, :, cols])

@@ -17,10 +17,9 @@ ROWS = 8
 N_TILE = ROWS * W
 BLOCKS = H // ROWS
 TILES = BLOCKS * PACK
-PIECE_ROWS = 4
-PIECES = H // PIECE_ROWS + 1
-STEPS_A_PIECE = 2
-LEAD = 5
+PIECE_ROWS = 2
+PIECES = (H + 2) // PIECE_ROWS
+LEAD = 9
 RIGHT_LAG = 2
 LEFT_LAG = 1
 GPSIMD_TILES = 3
@@ -82,9 +81,6 @@ def tile_staticgraphmodule_t_v_kernel(tc, x, Wp, b, z, grad_out, out):
         totals = {}
         shifteds = {}
 
-        def padded_rows(piece):
-            return max(PIECE_ROWS * piece - 2, 0), PIECE_ROWS * piece + 2
-
         def masked_gradient(dz_rows, at, row, n_rows):
             cols = slice(W * row, W * (row + n_rows))
             nc.vector.scalar_tensor_tensor(
@@ -97,27 +93,24 @@ def tile_staticgraphmodule_t_v_kernel(tc, x, Wp, b, z, grad_out, out):
             )
 
         def mask(piece):
-            rows = [min(max(r - 1, 0), H - 1) for r in range(*padded_rows(piece))]
             dz_rows = work.tile([P, PACK, PIECE_ROWS * W], BF16)
-            at = 0
-            while at < len(rows):
-                n_rows = 1
-                while at + n_rows < len(rows) and rows[at + n_rows] == rows[at] + n_rows:
-                    n_rows += 1
-                masked_gradient(dz_rows, at, rows[at], n_rows)
-                at += n_rows
-            dz = work.tile([P, PIECE_ROWS * W, PACK], BF16, align_bytes=64)
+            upper = min(max(PIECE_ROWS * piece - 1, 0), H - 1)
+            lower = min(PIECE_ROWS * piece, H - 1)
+            if lower == upper + 1:
+                masked_gradient(dz_rows, 0, upper, 2)
+            else:
+                masked_gradient(dz_rows, 0, upper, 1)
+                masked_gradient(dz_rows, 1, lower, 1)
+            dz = work.tile([P, PIECE_ROWS * W, PACK], BF16, align_bytes=64, bufs=4)
             masked[piece] = dz
-            width = W * len(rows)
-            nc.scalar.copy(out=dz[:, 0:width, :], in_=dz_rows[:, :, 0:width].rearrange("p t w -> p w t"))
+            nc.scalar.copy(out=dz[:], in_=dz_rows[:].rearrange("p t w -> p w t"))
 
         def quantise(piece):
-            first, end = padded_rows(piece)
-            cols = slice(W * first, W * end)
+            cols = slice(PIECE_ROWS * W * piece, PIECE_ROWS * W * (piece + 1))
             nc.vector.quantize_mx(
                 out=dq_codes[:, cols].bitcast(E5M2X4),
                 scales=dq_scales[:, cols],
-                in_=masked[piece][:, 0 : W * (end - first), :].rearrange("p w t -> p (w t)"),
+                in_=masked[piece][:].rearrange("p w t -> p (w t)"),
             )
 
         def multiply(acc, half, o, block, dy, start, stop):
@@ -206,17 +199,15 @@ def tile_staticgraphmodule_t_v_kernel(tc, x, Wp, b, z, grad_out, out):
                     in_=total[:].rearrange("p o r j -> p o (r j)"),
                 )
 
-        for n in range(-STEPS_A_PIECE * LEAD, TILES + RIGHT_LAG):
-            piece, phase = divmod(n, STEPS_A_PIECE)
-            piece += LEAD
+        for n in range(-LEAD, TILES + RIGHT_LAG):
             if 0 <= n < TILES:
                 products(n)
                 start_tile(n)
-            if phase == 0 and piece < PIECES:
-                mask(piece)
+            if n + LEAD < PIECES:
+                mask(n + LEAD)
+            if 0 <= n + LEAD - 2 < PIECES:
+                quantise(n + LEAD - 2)
             if 0 <= n - LEFT_LAG < TILES:
                 add_left_on_vector(n - LEFT_LAG)
             if 0 <= n - RIGHT_LAG:
                 finish_tile(n - RIGHT_LAG)
-            if phase == 0 and 0 <= piece - 1 < PIECES:
-                quantise(piece - 1)

@@ -13,16 +13,26 @@ PACK = 4
 C = 512
 H = 64
 W = 64
-ROWS = 8
-N_TILE = ROWS * W
-BLOCKS = H // ROWS
-TILES = BLOCKS * PACK
+BAND_ROWS = 8
+N_TILE = BAND_ROWS * W
+BANDS = H // BAND_ROWS
+TILES = BANDS * PACK
 PIECE_ROWS = 2
 PIECES = (H + 2) // PIECE_ROWS
+
 LEAD = 9
-RIGHT_LAG = 2
+QUANTISE_LAG = 2
 LEFT_LAG = 1
+RIGHT_LAG = 2
 GPSIMD_TILES = 3
+assert LEAD - QUANTISE_LAG > PACK
+
+PSUM_BANKS = 8
+VERT_BANKS = 5
+MID_BANKS = PSUM_BANKS - VERT_BANKS
+WORK_BUFS = 3
+DZ_BUFS = QUANTISE_LAG + 2
+RESULT_BUFS = 4
 
 FLOPS = 2 * C * (2 * C) * H * W
 BYTES = 2 * C * (2 * C) + (4 + 2 + 4) * C * H * W
@@ -37,57 +47,57 @@ def tile_staticgraphmodule_t_v_kernel(tc, x, Wp, b, z, grad_out, out):
 
     with (
         tc.tile_pool(name="keep", bufs=1) as keep,
-        tc.tile_pool(name="work", bufs=3) as work,
-        tc.tile_pool(name="result", bufs=4) as result,
-        tc.psum_pool(name="psum", bufs=4) as psum,
+        tc.tile_pool(name="work", bufs=WORK_BUFS) as work,
+        tc.tile_pool(name="result", bufs=RESULT_BUFS) as result,
+        tc.psum_pool(name="psum", bufs=PSUM_BANKS // 2) as psum,
         tc.manual_schedule(),
     ):
         w_raw = keep.tile([P, PACK, 2 * C], BF16)
         nc.sync.dma_start(out=w_raw[:], in_=w_rows)
         z_sb = keep.tile([P, PACK, H * W], F32)
         g_sb = keep.tile([P, PACK, H * W], BF16)
-        for block in range(BLOCKS):
-            first = 0 if block == 0 else ROWS * block + 1
-            last = min(ROWS * block + ROWS, H - 1)
-            cols = slice(W * first, W * (last + 1))
-            nc.sync.dma_start(out=z_sb[:, :, cols], in_=z_rows[:, :, cols])
-            nc.sync.dma_start(out=g_sb[:, :, cols], in_=g_rows[:, :, cols])
+        for band in range(BANDS):
+            first = 0 if band == 0 else BAND_ROWS * band + 1
+            last = min(BAND_ROWS * band + BAND_ROWS, H - 1)
+            positions = slice(W * first, W * (last + 1))
+            nc.sync.dma_start(out=z_sb[:, :, positions], in_=z_rows[:, :, positions])
+            nc.sync.dma_start(out=g_sb[:, :, positions], in_=g_rows[:, :, positions])
 
         w_grouped = keep.tile([P, 2 * C, PACK], BF16, align_bytes=64)
         w_codes = keep.tile([P, 2 * C], U32, align_bytes=64)
         w_scales = keep.tile([P, 2 * C], U8, align_bytes=64)
         nc.vector.tensor_copy(
-            out=w_grouped[:, 0:C, :].rearrange("p (o q) t -> p o q t", o=PACK),
-            in_=w_raw[:, :, 0:C].rearrange("p t (q o) -> p o q t", o=PACK),
+            out=w_grouped[:, 0:C, :].rearrange("p (c q) t -> p c q t", c=PACK),
+            in_=w_raw[:, :, 0:C].rearrange("p t (q c) -> p c q t", c=PACK),
         )
         nc.scalar.mul(
-            out=w_grouped[:, C : 2 * C, :].rearrange("p (o q) t -> p o q t", o=PACK),
-            in_=w_raw[:, :, C : 2 * C].rearrange("p t (q o) -> p o q t", o=PACK),
+            out=w_grouped[:, C : 2 * C, :].rearrange("p (c q) t -> p c q t", c=PACK),
+            in_=w_raw[:, :, C : 2 * C].rearrange("p t (q c) -> p c q t", c=PACK),
             mul=0.125,
         )
         for half in range(2):
-            m = slice(C * half, C * (half + 1))
+            w_cols = slice(C * half, C * (half + 1))
             nc.vector.quantize_mx(
-                out=w_codes[:, m].bitcast(E4M3X4),
-                scales=w_scales[:, m],
-                in_=w_grouped[:, m, :].rearrange("p m t -> p (m t)"),
+                out=w_codes[:, w_cols].bitcast(E4M3X4),
+                scales=w_scales[:, w_cols],
+                in_=w_grouped[:, w_cols, :].rearrange("p m t -> p (m t)"),
             )
 
         dq_codes = keep.tile([P, (H + 2) * W], U32, align_bytes=64)
         dq_scales = keep.tile([P, (H + 2) * W], U8, align_bytes=64)
-        masked = {}
+        regrouped = {}
         verts = {}
         mids = {}
         totals = {}
         shifteds = {}
 
         def masked_gradient(dz_rows, at, row, n_rows):
-            cols = slice(W * row, W * (row + n_rows))
+            positions = slice(W * row, W * (row + n_rows))
             nc.vector.scalar_tensor_tensor(
                 out=dz_rows[:, :, W * at : W * (at + n_rows)],
-                in0=z_sb[:, :, cols],
+                in0=z_sb[:, :, positions],
                 scalar=0.0,
-                in1=g_sb[:, :, cols],
+                in1=g_sb[:, :, positions],
                 op0=ALU.is_gt,
                 op1=ALU.mult,
             )
@@ -101,113 +111,125 @@ def tile_staticgraphmodule_t_v_kernel(tc, x, Wp, b, z, grad_out, out):
             else:
                 masked_gradient(dz_rows, 0, upper, 1)
                 masked_gradient(dz_rows, 1, lower, 1)
-            dz = work.tile([P, PIECE_ROWS * W, PACK], BF16, align_bytes=64, bufs=4)
-            masked[piece] = dz
+            dz = work.tile([P, PIECE_ROWS * W, PACK], BF16, align_bytes=64, bufs=DZ_BUFS)
+            regrouped[piece] = dz
             nc.scalar.copy(out=dz[:], in_=dz_rows[:].rearrange("p t w -> p w t"))
 
         def quantise(piece):
-            cols = slice(PIECE_ROWS * W * piece, PIECE_ROWS * W * (piece + 1))
+            padded = slice(PIECE_ROWS * W * piece, PIECE_ROWS * W * (piece + 1))
             nc.vector.quantize_mx(
-                out=dq_codes[:, cols].bitcast(E5M2X4),
-                scales=dq_scales[:, cols],
-                in_=masked[piece][:].rearrange("p w t -> p (w t)"),
+                out=dq_codes[:, padded].bitcast(E5M2X4),
+                scales=dq_scales[:, padded],
+                in_=regrouped[piece][:].rearrange("p w t -> p (w t)"),
             )
 
-        def multiply(acc, half, o, block, dy, start, stop):
-            m = slice(C * half + P * o, C * half + P * (o + 1))
-            first = W * (ROWS * block + 1 + dy)
+        def multiply(acc, half, c, band, dy, start, stop):
+            w_cols = slice(C * half + P * c, C * half + P * (c + 1))
+            window = W * (BAND_ROWS * band + 1 + dy)
             nc.tensor.matmul_mx(
                 out=acc[:].rearrange("p r j -> p (r j)"),
-                lhsT=w_codes[:, m].bitcast(E4M3X4),
-                lhsT_scale=w_scales[:, m],
-                rhs=dq_codes[:, first : first + N_TILE].bitcast(E5M2X4),
-                rhs_scale=dq_scales[:, first : first + N_TILE],
+                lhsT=w_codes[:, w_cols].bitcast(E4M3X4),
+                lhsT_scale=w_scales[:, w_cols],
+                rhs=dq_codes[:, window : window + N_TILE].bitcast(E5M2X4),
+                rhs_scale=dq_scales[:, window : window + N_TILE],
                 start=start,
                 stop=stop,
             )
 
         def products(n):
-            block, o = divmod(n, PACK)
-            vert = psum.tile([P, ROWS, W], F32, bufs=5)
-            multiply(vert, 1, o, block, -1, True, False)
-            multiply(vert, 1, o, block, 0, False, False)
-            multiply(vert, 1, o, block, 1, False, True)
-            mid = psum.tile([P, ROWS, W], F32, bufs=3)
-            multiply(mid, 1, o, block, -1, True, False)
-            multiply(mid, 1, o, block, 1, False, False)
-            multiply(mid, 0, o, block, 0, False, True)
+            band, c = divmod(n, PACK)
+            vert = psum.tile([P, BAND_ROWS, W], F32, bufs=VERT_BANKS)
+            multiply(vert, 1, c, band, -1, True, False)
+            multiply(vert, 1, c, band, 0, False, False)
+            multiply(vert, 1, c, band, 1, False, True)
+            mid = psum.tile([P, BAND_ROWS, W], F32, bufs=MID_BANKS)
+            multiply(mid, 1, c, band, -1, True, False)
+            multiply(mid, 1, c, band, 1, False, False)
+            multiply(mid, 0, c, band, 0, False, True)
             verts[n] = vert
             mids[n] = mid
 
         def start_tile(n):
-            block, o = divmod(n, PACK)
-            if o == 0:
-                total = result.tile([P, PACK, ROWS, W], F32)
-                shifted = work.tile([P, PACK, ROWS, W + 1], F32)
-                totals[block] = total
-                shifteds[block] = shifted
-            nc.scalar.copy(out=shifteds[block][:, o, :, 1 : W + 1], in_=verts[n][:])
-            nc.scalar.copy(out=shifteds[block][:, o, :, 0:1], in_=verts[n][:, :, 0:1])
+            band, c = divmod(n, PACK)
+            if c == 0:
+                total = result.tile([P, PACK, BAND_ROWS, W], F32)
+                shifted = work.tile([P, PACK, BAND_ROWS, W + 1], F32)
+                totals[band] = total
+                shifteds[band] = shifted
+            nc.scalar.copy(out=shifteds[band][:, c, :, 1 : W + 1], in_=verts[n][:])
+            nc.scalar.copy(out=shifteds[band][:, c, :, 0:1], in_=verts[n][:, :, 0:1])
             nc.vector.tensor_tensor(
-                out=totals[block][:, o, :, :],
+                out=totals[band][:, c, :, :],
                 in0=mids[n][:],
-                in1=g_sb[:, o, N_TILE * block : N_TILE * (block + 1)].rearrange("p (r j) -> p r j", j=W),
+                in1=g_sb[:, c, N_TILE * band : N_TILE * (band + 1)].rearrange("p (r j) -> p r j", j=W),
                 op=ALU.add,
             )
-            if o < GPSIMD_TILES:
+            if c < GPSIMD_TILES:
                 nc.gpsimd.tensor_tensor(
-                    out=totals[block][:, o, :, :],
-                    in0=totals[block][:, o, :, :],
-                    in1=shifteds[block][:, o, :, 0:W],
+                    out=totals[band][:, c, :, :],
+                    in0=totals[band][:, c, :, :],
+                    in1=shifteds[band][:, c, :, 0:W],
                     op=ALU.add,
                 )
 
         def add_left_on_vector(n):
-            block, o = divmod(n, PACK)
-            if o >= GPSIMD_TILES:
+            band, c = divmod(n, PACK)
+            if c >= GPSIMD_TILES:
                 nc.vector.tensor_tensor(
-                    out=totals[block][:, o, :, 1:W],
-                    in0=totals[block][:, o, :, 1:W],
+                    out=totals[band][:, c, :, 1:W],
+                    in0=totals[band][:, c, :, 1:W],
                     in1=verts[n][:, :, 0 : W - 1],
                     op=ALU.add,
                 )
 
-        def finish_tile(n):
-            block, o = divmod(n, PACK)
-            total = totals[block]
+        def add_edges(band):
+            total = totals[band]
             nc.vector.tensor_tensor(
-                out=total[:, o, :, 0 : W - 1],
-                in0=total[:, o, :, 0 : W - 1],
+                out=total[:, GPSIMD_TILES:PACK, :, 0:1],
+                in0=total[:, GPSIMD_TILES:PACK, :, 0:1],
+                in1=shifteds[band][:, GPSIMD_TILES:PACK, :, 0:1],
+                op=ALU.add,
+            )
+            nc.vector.tensor_tensor(
+                out=total[:, :, :, W - 1 : W],
+                in0=total[:, :, :, W - 1 : W],
+                in1=shifteds[band][:, :, :, W : W + 1],
+                op=ALU.add,
+            )
+
+        def add_right(n):
+            band, c = divmod(n, PACK)
+            nc.vector.tensor_tensor(
+                out=totals[band][:, c, :, 0 : W - 1],
+                in0=totals[band][:, c, :, 0 : W - 1],
                 in1=verts[n][:, :, 1:W],
                 op=ALU.add,
             )
-            if o == PACK - 1:
-                nc.vector.tensor_tensor(
-                    out=total[:, GPSIMD_TILES:PACK, :, 0:1],
-                    in0=total[:, GPSIMD_TILES:PACK, :, 0:1],
-                    in1=shifteds[block][:, GPSIMD_TILES:PACK, :, 0:1],
-                    op=ALU.add,
-                )
-                nc.vector.tensor_tensor(
-                    out=total[:, :, :, W - 1 : W],
-                    in0=total[:, :, :, W - 1 : W],
-                    in1=shifteds[block][:, :, :, W : W + 1],
-                    op=ALU.add,
-                )
-                nc.sync.dma_start(
-                    out=out_rows[:, :, N_TILE * block : N_TILE * (block + 1)],
-                    in_=total[:].rearrange("p o r j -> p o (r j)"),
-                )
+
+        def store(n):
+            band, c = divmod(n, PACK)
+            nc.sync.dma_start(
+                out=out_rows[:, c, N_TILE * band : N_TILE * (band + 1)],
+                in_=totals[band][:, c, :, :].rearrange("p r j -> p (r j)"),
+            )
 
         for n in range(-LEAD, TILES + RIGHT_LAG):
+            ending = n - RIGHT_LAG
+            ends_band = ending >= 0 and ending % PACK == PACK - 1
             if 0 <= n < TILES:
                 products(n)
                 start_tile(n)
             if n + LEAD < PIECES:
                 mask(n + LEAD)
-            if 0 <= n + LEAD - 2 < PIECES:
-                quantise(n + LEAD - 2)
+            if 0 <= n + LEAD - QUANTISE_LAG < PIECES:
+                quantise(n + LEAD - QUANTISE_LAG)
+            if ends_band:
+                add_edges(ending // PACK)
+                for complete in range(ending - PACK + 1, ending):
+                    store(complete)
             if 0 <= n - LEFT_LAG < TILES:
                 add_left_on_vector(n - LEFT_LAG)
-            if 0 <= n - RIGHT_LAG:
-                finish_tile(n - RIGHT_LAG)
+            if ending >= 0:
+                add_right(ending)
+            if ends_band:
+                store(ending)

@@ -24,7 +24,7 @@ LEAD = 9
 QUANTISE_LAG = 2
 LEFT_LAG = 1
 RIGHT_LAG = 2
-GPSIMD_TILES = 3
+GPSIMD_TILES = 4
 assert LEAD - QUANTISE_LAG > PACK
 
 PSUM_BANKS = 8
@@ -184,12 +184,13 @@ def tile_staticgraphmodule_t_v_kernel(tc, x, Wp, b, z, grad_out, out):
 
         def add_edges(band):
             total = totals[band]
-            nc.vector.tensor_tensor(
-                out=total[:, GPSIMD_TILES:PACK, :, 0:1],
-                in0=total[:, GPSIMD_TILES:PACK, :, 0:1],
-                in1=shifteds[band][:, GPSIMD_TILES:PACK, :, 0:1],
-                op=ALU.add,
-            )
+            if GPSIMD_TILES < PACK:
+                nc.vector.tensor_tensor(
+                    out=total[:, GPSIMD_TILES:PACK, :, 0:1],
+                    in0=total[:, GPSIMD_TILES:PACK, :, 0:1],
+                    in1=shifteds[band][:, GPSIMD_TILES:PACK, :, 0:1],
+                    op=ALU.add,
+                )
             nc.vector.tensor_tensor(
                 out=total[:, :, :, W - 1 : W],
                 in0=total[:, :, :, W - 1 : W],

@@ -22,9 +22,8 @@ PIECES = (H + 2) // PIECE_ROWS
 
 LEAD = 9
 QUANTISE_LAG = 2
-LEFT_LAG = 1
 RIGHT_LAG = 2
-GPSIMD_TILES = 4
+LAST_TILE = TILES - 1
 assert LEAD - QUANTISE_LAG > PACK
 
 PSUM_BANKS = 8
@@ -138,16 +137,27 @@ def tile_staticgraphmodule_t_v_kernel(tc, x, Wp, b, z, grad_out, out):
 
         def products(n):
             band, c = divmod(n, PACK)
-            vert = psum.tile([P, BAND_ROWS, W], F32, bufs=VERT_BANKS)
-            multiply(vert, 1, c, band, -1, True, False)
-            multiply(vert, 1, c, band, 0, False, False)
-            multiply(vert, 1, c, band, 1, False, True)
-            mid = psum.tile([P, BAND_ROWS, W], F32, bufs=MID_BANKS)
-            multiply(mid, 1, c, band, -1, True, False)
-            multiply(mid, 1, c, band, 1, False, False)
-            multiply(mid, 0, c, band, 0, False, True)
-            verts[n] = vert
-            mids[n] = mid
+
+            def vert_passes():
+                vert = psum.tile([P, BAND_ROWS, W], F32, name="vert", bufs=VERT_BANKS)
+                multiply(vert, 1, c, band, -1, True, False)
+                multiply(vert, 1, c, band, 0, False, False)
+                multiply(vert, 1, c, band, 1, False, True)
+                verts[n] = vert
+
+            def mid_passes():
+                mid = psum.tile([P, BAND_ROWS, W], F32, name="mid", bufs=MID_BANKS)
+                multiply(mid, 1, c, band, -1, True, False)
+                multiply(mid, 1, c, band, 1, False, False)
+                multiply(mid, 0, c, band, 0, False, True)
+                mids[n] = mid
+
+            if n == LAST_TILE:
+                mid_passes()
+                vert_passes()
+            else:
+                vert_passes()
+                mid_passes()
 
         def start_tile(n):
             band, c = divmod(n, PACK)
@@ -156,15 +166,16 @@ def tile_staticgraphmodule_t_v_kernel(tc, x, Wp, b, z, grad_out, out):
                 shifted = work.tile([P, PACK, BAND_ROWS, W + 1], F32)
                 totals[band] = total
                 shifteds[band] = shifted
-            nc.scalar.copy(out=shifteds[band][:, c, :, 1 : W + 1], in_=verts[n][:])
-            nc.scalar.copy(out=shifteds[band][:, c, :, 0:1], in_=verts[n][:, :, 0:1])
+            if n != LAST_TILE:
+                nc.scalar.copy(out=shifteds[band][:, c, :, 1 : W + 1], in_=verts[n][:])
+                nc.scalar.copy(out=shifteds[band][:, c, :, 0:1], in_=verts[n][:, :, 0:1])
             nc.vector.tensor_tensor(
                 out=totals[band][:, c, :, :],
                 in0=mids[n][:],
                 in1=g_sb[:, c, N_TILE * band : N_TILE * (band + 1)].rearrange("p (r j) -> p r j", j=W),
                 op=ALU.add,
             )
-            if c < GPSIMD_TILES:
+            if n != LAST_TILE:
                 nc.gpsimd.tensor_tensor(
                     out=totals[band][:, c, :, :],
                     in0=totals[band][:, c, :, :],
@@ -172,29 +183,11 @@ def tile_staticgraphmodule_t_v_kernel(tc, x, Wp, b, z, grad_out, out):
                     op=ALU.add,
                 )
 
-        def add_left_on_vector(n):
-            band, c = divmod(n, PACK)
-            if c >= GPSIMD_TILES:
-                nc.vector.tensor_tensor(
-                    out=totals[band][:, c, :, 1:W],
-                    in0=totals[band][:, c, :, 1:W],
-                    in1=verts[n][:, :, 0 : W - 1],
-                    op=ALU.add,
-                )
-
-        def add_edges(band):
-            total = totals[band]
-            if GPSIMD_TILES < PACK:
-                nc.vector.tensor_tensor(
-                    out=total[:, GPSIMD_TILES:PACK, :, 0:1],
-                    in0=total[:, GPSIMD_TILES:PACK, :, 0:1],
-                    in1=shifteds[band][:, GPSIMD_TILES:PACK, :, 0:1],
-                    op=ALU.add,
-                )
+        def add_right_edges(band, tiles):
             nc.vector.tensor_tensor(
-                out=total[:, :, :, W - 1 : W],
-                in0=total[:, :, :, W - 1 : W],
-                in1=shifteds[band][:, :, :, W : W + 1],
+                out=totals[band][:, 0:tiles, :, W - 1 : W],
+                in0=totals[band][:, 0:tiles, :, W - 1 : W],
+                in1=shifteds[band][:, 0:tiles, :, W : W + 1],
                 op=ALU.add,
             )
 
@@ -206,6 +199,21 @@ def tile_staticgraphmodule_t_v_kernel(tc, x, Wp, b, z, grad_out, out):
                 in1=verts[n][:, :, 1:W],
                 op=ALU.add,
             )
+
+        def finish_last_tile():
+            band, c = divmod(LAST_TILE, PACK)
+            total = totals[band]
+            vert = verts[LAST_TILE]
+            nc.vector.tensor_tensor(
+                out=total[:, c, :, 1:W], in0=total[:, c, :, 1:W], in1=vert[:, :, 0 : W - 1], op=ALU.add
+            )
+            nc.vector.tensor_tensor(
+                out=total[:, c, :, 0 : W : W - 1],
+                in0=total[:, c, :, 0 : W : W - 1],
+                in1=vert[:, :, 0 : W : W - 1],
+                op=ALU.add,
+            )
+            add_right(LAST_TILE)
 
         def store(n):
             band, c = divmod(n, PACK)
@@ -224,13 +232,18 @@ def tile_staticgraphmodule_t_v_kernel(tc, x, Wp, b, z, grad_out, out):
                 mask(n + LEAD)
             if 0 <= n + LEAD - QUANTISE_LAG < PIECES:
                 quantise(n + LEAD - QUANTISE_LAG)
-            if ends_band:
-                add_edges(ending // PACK)
+            if ends_band and ending != LAST_TILE:
+                add_right_edges(ending // PACK, PACK)
                 for complete in range(ending - PACK + 1, ending):
                     store(complete)
-            if 0 <= n - LEFT_LAG < TILES:
-                add_left_on_vector(n - LEFT_LAG)
-            if ending >= 0:
+            if 0 <= ending < LAST_TILE:
                 add_right(ending)
-            if ends_band:
+            if ends_band and ending != LAST_TILE:
+                store(ending)
+            if ending == LAST_TILE - 1:
+                add_right_edges(ending // PACK, PACK - 1)
+                for complete in range(ending - PACK + 2, ending + 1):
+                    store(complete)
+            if ending == LAST_TILE:
+                finish_last_tile()
                 store(ending)

@@ -7,6 +7,7 @@ U8 = mybir.dt.uint8
 E4M3X4 = mybir.dt.float8_e4m3fn_x4
 E5M2X4 = mybir.dt.float8_e5m2_x4
 ALU = mybir.AluOpType
+ACT = mybir.ActivationFunctionType
 
 P = 128
 PACK = 4
@@ -22,6 +23,8 @@ PIECES = (H + 2) // PIECE_ROWS
 
 LEAD = 9
 QUANTISE_LAG = 2
+SIGN_FROM = 13
+SIGN_LEAD = 2
 RIGHT_LAG = 2
 LAST_TILE = TILES - 1
 assert LEAD - QUANTISE_LAG > PACK
@@ -30,6 +33,7 @@ PSUM_BANKS = 8
 VERT_BANKS = 5
 MID_BANKS = PSUM_BANKS - VERT_BANKS
 WORK_BUFS = 3
+SIGN_BUFS = SIGN_LEAD + 2
 DZ_BUFS = QUANTISE_LAG + 2
 RESULT_BUFS = 4
 
@@ -84,6 +88,7 @@ def tile_staticgraphmodule_t_v_kernel(tc, x, Wp, b, z, grad_out, out):
 
         dq_codes = keep.tile([P, (H + 2) * W], U32, align_bytes=64)
         dq_scales = keep.tile([P, (H + 2) * W], U8, align_bytes=64)
+        positive = {}
         regrouped = {}
         verts = {}
         mids = {}
@@ -101,11 +106,30 @@ def tile_staticgraphmodule_t_v_kernel(tc, x, Wp, b, z, grad_out, out):
                 op1=ALU.mult,
             )
 
+        def by_sign(piece):
+            return SIGN_FROM <= piece < PIECES - 1
+
+        def sign(piece):
+            first = PIECE_ROWS * piece - 1
+            ones = work.tile([P, PACK, PIECE_ROWS * W], BF16, bufs=SIGN_BUFS)
+            positive[piece] = ones
+            nc.scalar.activation(out=ones[:], in_=z_sb[:, :, W * first : W * (first + PIECE_ROWS)], func=ACT.Sign)
+
+        def clip(piece):
+            nc.vector.tensor_scalar_max(out=positive[piece][:], in0=positive[piece][:], scalar1=0.0)
+
         def mask(piece):
             dz_rows = work.tile([P, PACK, PIECE_ROWS * W], BF16)
             upper = min(max(PIECE_ROWS * piece - 1, 0), H - 1)
             lower = min(PIECE_ROWS * piece, H - 1)
-            if lower == upper + 1:
+            if by_sign(piece):
+                nc.vector.tensor_tensor(
+                    out=dz_rows[:],
+                    in0=positive[piece][:],
+                    in1=g_sb[:, :, W * upper : W * (upper + PIECE_ROWS)],
+                    op=ALU.mult,
+                )
+            elif lower == upper + 1:
                 masked_gradient(dz_rows, 0, upper, 2)
             else:
                 masked_gradient(dz_rows, 0, upper, 1)
@@ -228,6 +252,10 @@ def tile_staticgraphmodule_t_v_kernel(tc, x, Wp, b, z, grad_out, out):
             if 0 <= n < TILES:
                 products(n)
                 start_tile(n)
+            if by_sign(n + LEAD + SIGN_LEAD):
+                sign(n + LEAD + SIGN_LEAD)
+            if by_sign(n + LEAD + 1):
+                clip(n + LEAD + 1)
             if n + LEAD < PIECES:
                 mask(n + LEAD)
             if 0 <= n + LEAD - QUANTISE_LAG < PIECES:

@@ -26,6 +26,8 @@ QUANTISE_LAG = 2
 SIGN_FROM = 13
 SIGN_LEAD = 2
 RIGHT_LAG = 2
+LAST_BAND = BANDS - 1
+LAST_FIRST = PACK * LAST_BAND
 LAST_TILE = TILES - 1
 assert LEAD - QUANTISE_LAG > PACK
 
@@ -159,53 +161,56 @@ def tile_staticgraphmodule_t_v_kernel(tc, x, Wp, b, z, grad_out, out):
                 stop=stop,
             )
 
-        def products(n):
+        def vert_passes(n):
             band, c = divmod(n, PACK)
+            vert = psum.tile([P, BAND_ROWS, W], F32, name="vert", bufs=VERT_BANKS)
+            multiply(vert, 1, c, band, -1, True, False)
+            multiply(vert, 1, c, band, 0, False, False)
+            multiply(vert, 1, c, band, 1, False, True)
+            verts[n] = vert
 
-            def vert_passes():
-                vert = psum.tile([P, BAND_ROWS, W], F32, name="vert", bufs=VERT_BANKS)
-                multiply(vert, 1, c, band, -1, True, False)
-                multiply(vert, 1, c, band, 0, False, False)
-                multiply(vert, 1, c, band, 1, False, True)
-                verts[n] = vert
-
-            def mid_passes():
-                mid = psum.tile([P, BAND_ROWS, W], F32, name="mid", bufs=MID_BANKS)
-                multiply(mid, 1, c, band, -1, True, False)
-                multiply(mid, 1, c, band, 1, False, False)
-                multiply(mid, 0, c, band, 0, False, True)
-                mids[n] = mid
-
+        def mid_passes(n):
+            band, c = divmod(n, PACK)
             if n == LAST_TILE:
-                mid_passes()
-                vert_passes()
+                mid = psum.tile([P, BAND_ROWS, W], F32, name="vert", bufs=VERT_BANKS)
             else:
-                vert_passes()
-                mid_passes()
+                mid = psum.tile([P, BAND_ROWS, W], F32, name="mid", bufs=MID_BANKS)
+            multiply(mid, 1, c, band, -1, True, False)
+            multiply(mid, 1, c, band, 1, False, False)
+            multiply(mid, 0, c, band, 0, False, True)
+            mids[n] = mid
+
+        def band_tiles(band):
+            total = result.tile([P, PACK, BAND_ROWS, W], F32)
+            shifted = work.tile([P, PACK, BAND_ROWS, W + 1], F32)
+            totals[band] = total
+            shifteds[band] = shifted
+
+        def gradient(n):
+            band, c = divmod(n, PACK)
+            return g_sb[:, c, N_TILE * band : N_TILE * (band + 1)].rearrange("p (r j) -> p r j", j=W)
+
+        def copy_vert(n):
+            band, c = divmod(n, PACK)
+            nc.scalar.copy(out=shifteds[band][:, c, :, 1 : W + 1], in_=verts[n][:])
+            nc.scalar.copy(out=shifteds[band][:, c, :, 0:1], in_=verts[n][:, :, 0:1])
+
+        def add_left(n):
+            band, c = divmod(n, PACK)
+            nc.gpsimd.tensor_tensor(
+                out=totals[band][:, c, :, :],
+                in0=totals[band][:, c, :, :],
+                in1=shifteds[band][:, c, :, 0:W],
+                op=ALU.add,
+            )
 
         def start_tile(n):
             band, c = divmod(n, PACK)
             if c == 0:
-                total = result.tile([P, PACK, BAND_ROWS, W], F32)
-                shifted = work.tile([P, PACK, BAND_ROWS, W + 1], F32)
-                totals[band] = total
-                shifteds[band] = shifted
-            if n != LAST_TILE:
-                nc.scalar.copy(out=shifteds[band][:, c, :, 1 : W + 1], in_=verts[n][:])
-                nc.scalar.copy(out=shifteds[band][:, c, :, 0:1], in_=verts[n][:, :, 0:1])
-            nc.vector.tensor_tensor(
-                out=totals[band][:, c, :, :],
-                in0=mids[n][:],
-                in1=g_sb[:, c, N_TILE * band : N_TILE * (band + 1)].rearrange("p (r j) -> p r j", j=W),
-                op=ALU.add,
-            )
-            if n != LAST_TILE:
-                nc.gpsimd.tensor_tensor(
-                    out=totals[band][:, c, :, :],
-                    in0=totals[band][:, c, :, :],
-                    in1=shifteds[band][:, c, :, 0:W],
-                    op=ALU.add,
-                )
+                band_tiles(band)
+            copy_vert(n)
+            nc.vector.tensor_tensor(out=totals[band][:, c, :, :], in0=mids[n][:], in1=gradient(n), op=ALU.add)
+            add_left(n)
 
         def add_right_edges(band, tiles):
             nc.vector.tensor_tensor(
@@ -224,21 +229,6 @@ def tile_staticgraphmodule_t_v_kernel(tc, x, Wp, b, z, grad_out, out):
                 op=ALU.add,
             )
 
-        def finish_last_tile():
-            band, c = divmod(LAST_TILE, PACK)
-            total = totals[band]
-            vert = verts[LAST_TILE]
-            nc.vector.tensor_tensor(
-                out=total[:, c, :, 1:W], in0=total[:, c, :, 1:W], in1=vert[:, :, 0 : W - 1], op=ALU.add
-            )
-            nc.vector.tensor_tensor(
-                out=total[:, c, :, 0 : W : W - 1],
-                in0=total[:, c, :, 0 : W : W - 1],
-                in1=vert[:, :, 0 : W : W - 1],
-                op=ALU.add,
-            )
-            add_right(LAST_TILE)
-
         def store(n):
             band, c = divmod(n, PACK)
             nc.sync.dma_start(
@@ -246,12 +236,24 @@ def tile_staticgraphmodule_t_v_kernel(tc, x, Wp, b, z, grad_out, out):
                 in_=totals[band][:, c, :, :].rearrange("p r j -> p (r j)"),
             )
 
-        for n in range(-LEAD, TILES + RIGHT_LAG):
+        def add_mid(n):
+            band, c = divmod(n, PACK)
+            nc.vector.tensor_tensor(
+                out=totals[band][:, c, :, :], in0=totals[band][:, c, :, :], in1=mids[n][:], op=ALU.add
+            )
+            store(n)
+
+        for n in range(-LEAD, LAST_FIRST):
             ending = n - RIGHT_LAG
             ends_band = ending >= 0 and ending % PACK == PACK - 1
-            if 0 <= n < TILES:
-                products(n)
+            if 0 <= n < LAST_FIRST:
+                vert_passes(n)
+                mid_passes(n)
                 start_tile(n)
+            if LAST_FIRST - PACK <= n < LAST_FIRST:
+                if n == LAST_FIRST - PACK:
+                    band_tiles(LAST_BAND)
+                nc.scalar.copy(out=totals[LAST_BAND][:, n + PACK - LAST_FIRST, :, :], in_=gradient(n + PACK))
             if by_sign(n + LEAD + SIGN_LEAD):
                 sign(n + LEAD + SIGN_LEAD)
             if by_sign(n + LEAD + 1):
@@ -260,18 +262,54 @@ def tile_staticgraphmodule_t_v_kernel(tc, x, Wp, b, z, grad_out, out):
                 mask(n + LEAD)
             if 0 <= n + LEAD - QUANTISE_LAG < PIECES:
                 quantise(n + LEAD - QUANTISE_LAG)
-            if ends_band and ending != LAST_TILE:
+            if ends_band:
                 add_right_edges(ending // PACK, PACK)
                 for complete in range(ending - PACK + 1, ending):
                     store(complete)
-            if 0 <= ending < LAST_TILE:
+            if 0 <= ending:
                 add_right(ending)
-            if ends_band and ending != LAST_TILE:
+            if ends_band:
                 store(ending)
-            if ending == LAST_TILE - 1:
-                add_right_edges(ending // PACK, PACK - 1)
-                for complete in range(ending - PACK + 2, ending + 1):
-                    store(complete)
-            if ending == LAST_TILE:
-                finish_last_tile()
-                store(ending)
+
+        first = LAST_FIRST
+
+        def neighbours(n):
+            c = n - first
+            add_right(n)
+            nc.vector.tensor_tensor(
+                out=totals[LAST_BAND][:, c, :, W - 1 : W],
+                in0=totals[LAST_BAND][:, c, :, W - 1 : W],
+                in1=shifteds[LAST_BAND][:, c, :, W : W + 1],
+                op=ALU.add,
+            )
+            add_left(n)
+
+        vert_passes(first)
+        copy_vert(first)
+        add_right(first - 2)
+        neighbours(first)
+        vert_passes(first + 1)
+        copy_vert(first + 1)
+        add_right_edges(LAST_BAND - 1, PACK)
+        for complete in range(first - PACK, first - 1):
+            store(complete)
+        add_right(first - 1)
+        store(first - 1)
+        neighbours(first + 1)
+        vert_passes(first + 2)
+        copy_vert(first + 2)
+        neighbours(first + 2)
+        vert_passes(LAST_TILE)
+        last = totals[LAST_BAND][:, PACK - 1, :, :]
+        last_vert = verts[LAST_TILE]
+        for n in range(first, TILES):
+            mid_passes(n)
+        nc.vector.tensor_tensor(out=last[:, :, 1:W], in0=last[:, :, 1:W], in1=last_vert[:, :, 0 : W - 1], op=ALU.add)
+        add_mid(first)
+        add_right(LAST_TILE)
+        add_mid(first + 1)
+        nc.vector.tensor_tensor(
+            out=last[:, :, 0 : W : W - 1], in0=last[:, :, 0 : W : W - 1], in1=last_vert[:, :, 0 : W : W - 1], op=ALU.add
+        )
+        add_mid(first + 2)
+        add_mid(LAST_TILE)

@@ -250,10 +250,6 @@ def tile_staticgraphmodule_t_v_kernel(tc, x, Wp, b, z, grad_out, out):
                 vert_passes(n)
                 mid_passes(n)
                 start_tile(n)
-            if LAST_FIRST - PACK <= n < LAST_FIRST:
-                if n == LAST_FIRST - PACK:
-                    band_tiles(LAST_BAND)
-                nc.scalar.copy(out=totals[LAST_BAND][:, n + PACK - LAST_FIRST, :, :], in_=gradient(n + PACK))
             if by_sign(n + LEAD + SIGN_LEAD):
                 sign(n + LEAD + SIGN_LEAD)
             if by_sign(n + LEAD + 1):
@@ -272,14 +268,23 @@ def tile_staticgraphmodule_t_v_kernel(tc, x, Wp, b, z, grad_out, out):
                 store(ending)
 
         first = LAST_FIRST
+        band_tiles(LAST_BAND)
+
+        def right_and_gradient(n):
+            nc.vector.tensor_tensor(
+                out=totals[LAST_BAND][:, n - first, :, 0 : W - 1],
+                in0=verts[n][:, :, 1:W],
+                in1=gradient(n)[:, :, 0 : W - 1],
+                op=ALU.add,
+            )
 
         def neighbours(n):
             c = n - first
-            add_right(n)
+            right_and_gradient(n)
             nc.vector.tensor_tensor(
                 out=totals[LAST_BAND][:, c, :, W - 1 : W],
-                in0=totals[LAST_BAND][:, c, :, W - 1 : W],
-                in1=shifteds[LAST_BAND][:, c, :, W : W + 1],
+                in0=shifteds[LAST_BAND][:, c, :, W : W + 1],
+                in1=gradient(n)[:, :, W - 1 : W],
                 op=ALU.add,
             )
             add_left(n)
@@ -304,12 +309,16 @@ def tile_staticgraphmodule_t_v_kernel(tc, x, Wp, b, z, grad_out, out):
         last_vert = verts[LAST_TILE]
         for n in range(first, TILES):
             mid_passes(n)
-        nc.vector.tensor_tensor(out=last[:, :, 1:W], in0=last[:, :, 1:W], in1=last_vert[:, :, 0 : W - 1], op=ALU.add)
-        add_mid(first)
-        add_right(LAST_TILE)
-        add_mid(first + 1)
+        right_and_gradient(LAST_TILE)
         nc.vector.tensor_tensor(
-            out=last[:, :, 0 : W : W - 1], in0=last[:, :, 0 : W : W - 1], in1=last_vert[:, :, 0 : W : W - 1], op=ALU.add
+            out=last[:, :, W - 1 : W],
+            in0=last_vert[:, :, W - 1 : W],
+            in1=gradient(LAST_TILE)[:, :, W - 1 : W],
+            op=ALU.add,
         )
+        add_mid(first)
+        nc.vector.tensor_tensor(out=last[:, :, 1:W], in0=last[:, :, 1:W], in1=last_vert[:, :, 0 : W - 1], op=ALU.add)
+        add_mid(first + 1)
+        nc.vector.tensor_tensor(out=last[:, :, 0:1], in0=last[:, :, 0:1], in1=last_vert[:, :, 0:1], op=ALU.add)
         add_mid(first + 2)
         add_mid(LAST_TILE)

import concourse.mybir as mybir

F32 = mybir.dt.float32
BF16 = mybir.dt.bfloat16
U32 = mybir.dt.uint32
U8 = mybir.dt.uint8
E4M3X4 = mybir.dt.float8_e4m3fn_x4
E5M2X4 = mybir.dt.float8_e5m2_x4
ALU = mybir.AluOpType
ACT = mybir.ActivationFunctionType

P = 128
PACK = 4
C = 512
H = 64
W = 64
BAND_ROWS = 8
N_TILE = BAND_ROWS * W
BANDS = H // BAND_ROWS
TILES = BANDS * PACK
PIECE_ROWS = 2
PIECES = (H + 2) // PIECE_ROWS

LEAD = 9
QUANTISE_LAG = 2
SIGN_FROM = 13
SIGN_LEAD = 2
RIGHT_LAG = 2
LAST_BAND = BANDS - 1
LAST_FIRST = PACK * LAST_BAND
LAST_TILE = TILES - 1
assert LEAD - QUANTISE_LAG > PACK

PSUM_BANKS = 8
VERT_BANKS = 5
MID_BANKS = PSUM_BANKS - VERT_BANKS
WORK_BUFS = 3
SIGN_BUFS = SIGN_LEAD + 2
DZ_BUFS = QUANTISE_LAG + 2
RESULT_BUFS = 4

FLOPS = 2 * C * (2 * C) * H * W
BYTES = 2 * C * (2 * C) + (4 + 2 + 4) * C * H * W


def tile_staticgraphmodule_t_v_kernel(tc, x, Wp, b, z, grad_out, out):
    nc = tc.nc
    z_rows = z.rearrange("n (p t) h w -> (n p) t (h w)", t=PACK)
    g_rows = grad_out.rearrange("n (p t) h w -> (n p) t (h w)", t=PACK)
    out_rows = out.rearrange("n (p t) h w -> (n p) t (h w)", t=PACK)
    w_rows = Wp.rearrange("(p t) m -> p t m", t=PACK)

    with (
        tc.tile_pool(name="keep", bufs=1) as keep,
        tc.tile_pool(name="work", bufs=WORK_BUFS) as work,
        tc.tile_pool(name="result", bufs=RESULT_BUFS) as result,
        tc.psum_pool(name="psum", bufs=PSUM_BANKS // 2) as psum,
        tc.manual_schedule(),
    ):
        w_raw = keep.tile([P, PACK, 2 * C], BF16)
        nc.sync.dma_start(out=w_raw[:], in_=w_rows)
        z_sb = keep.tile([P, PACK, H * W], F32)
        g_sb = keep.tile([P, PACK, H * W], BF16)
        for band in range(BANDS):
            first = 0 if band == 0 else BAND_ROWS * band + 1
            last = min(BAND_ROWS * band + BAND_ROWS, H - 1)
            positions = slice(W * first, W * (last + 1))
            nc.sync.dma_start(out=z_sb[:, :, positions], in_=z_rows[:, :, positions])
            nc.sync.dma_start(out=g_sb[:, :, positions], in_=g_rows[:, :, positions])

        w_grouped = keep.tile([P, 2 * C, PACK], BF16, align_bytes=64)
        w_codes = keep.tile([P, 2 * C], U32, align_bytes=64)
        w_scales = keep.tile([P, 2 * C], U8, align_bytes=64)
        nc.vector.tensor_copy(
            out=w_grouped[:, 0:C, :].rearrange("p (c q) t -> p c q t", c=PACK),
            in_=w_raw[:, :, 0:C].rearrange("p t (q c) -> p c q t", c=PACK),
        )
        nc.scalar.mul(
            out=w_grouped[:, C : 2 * C, :].rearrange("p (c q) t -> p c q t", c=PACK),
            in_=w_raw[:, :, C : 2 * C].rearrange("p t (q c) -> p c q t", c=PACK),
            mul=0.125,
        )
        for half in range(2):
            w_cols = slice(C * half, C * (half + 1))
            nc.vector.quantize_mx(
                out=w_codes[:, w_cols].bitcast(E4M3X4),
                scales=w_scales[:, w_cols],
                in_=w_grouped[:, w_cols, :].rearrange("p m t -> p (m t)"),
            )

        dq_codes = keep.tile([P, (H + 2) * W], U32, align_bytes=64)
        dq_scales = keep.tile([P, (H + 2) * W], U8, align_bytes=64)
        positive = {}
        regrouped = {}
        verts = {}
        mids = {}
        totals = {}
        shifteds = {}

        def masked_gradient(dz_rows, at, row, n_rows):
            positions = slice(W * row, W * (row + n_rows))
            nc.vector.scalar_tensor_tensor(
                out=dz_rows[:, :, W * at : W * (at + n_rows)],
                in0=z_sb[:, :, positions],
                scalar=0.0,
                in1=g_sb[:, :, positions],
                op0=ALU.is_gt,
                op1=ALU.mult,
            )

        def by_sign(piece):
            return SIGN_FROM <= piece < PIECES - 1

        def sign(piece):
            first = PIECE_ROWS * piece - 1
            ones = work.tile([P, PACK, PIECE_ROWS * W], BF16, bufs=SIGN_BUFS)
            positive[piece] = ones
            nc.scalar.activation(out=ones[:], in_=z_sb[:, :, W * first : W * (first + PIECE_ROWS)], func=ACT.Sign)

        def clip(piece):
            nc.vector.tensor_scalar_max(out=positive[piece][:], in0=positive[piece][:], scalar1=0.0)

        def mask(piece):
            dz_rows = work.tile([P, PACK, PIECE_ROWS * W], BF16)
            upper = min(max(PIECE_ROWS * piece - 1, 0), H - 1)
            lower = min(PIECE_ROWS * piece, H - 1)
            if by_sign(piece):
                nc.vector.tensor_tensor(
                    out=dz_rows[:],
                    in0=positive[piece][:],
                    in1=g_sb[:, :, W * upper : W * (upper + PIECE_ROWS)],
                    op=ALU.mult,
                )
            elif lower == upper + 1:
                masked_gradient(dz_rows, 0, upper, 2)
            else:
                masked_gradient(dz_rows, 0, upper, 1)
                masked_gradient(dz_rows, 1, lower, 1)
            dz = work.tile([P, PIECE_ROWS * W, PACK], BF16, align_bytes=64, bufs=DZ_BUFS)
            regrouped[piece] = dz
            nc.scalar.copy(out=dz[:], in_=dz_rows[:].rearrange("p t w -> p w t"))

        def quantise(piece):
            padded = slice(PIECE_ROWS * W * piece, PIECE_ROWS * W * (piece + 1))
            nc.vector.quantize_mx(
                out=dq_codes[:, padded].bitcast(E5M2X4),
                scales=dq_scales[:, padded],
                in_=regrouped[piece][:].rearrange("p w t -> p (w t)"),
            )

        def multiply(acc, half, c, band, dy, start, stop):
            w_cols = slice(C * half + P * c, C * half + P * (c + 1))
            window = W * (BAND_ROWS * band + 1 + dy)
            nc.tensor.matmul_mx(
                out=acc[:].rearrange("p r j -> p (r j)"),
                lhsT=w_codes[:, w_cols].bitcast(E4M3X4),
                lhsT_scale=w_scales[:, w_cols],
                rhs=dq_codes[:, window : window + N_TILE].bitcast(E5M2X4),
                rhs_scale=dq_scales[:, window : window + N_TILE],
                start=start,
                stop=stop,
            )

        def vert_passes(n):
            band, c = divmod(n, PACK)
            vert = psum.tile([P, BAND_ROWS, W], F32, name="vert", bufs=VERT_BANKS)
            multiply(vert, 1, c, band, -1, True, False)
            multiply(vert, 1, c, band, 0, False, False)
            multiply(vert, 1, c, band, 1, False, True)
            verts[n] = vert

        def mid_passes(n):
            band, c = divmod(n, PACK)
            if n == LAST_TILE:
                mid = psum.tile([P, BAND_ROWS, W], F32, name="vert", bufs=VERT_BANKS)
            else:
                mid = psum.tile([P, BAND_ROWS, W], F32, name="mid", bufs=MID_BANKS)
            multiply(mid, 1, c, band, -1, True, False)
            multiply(mid, 1, c, band, 1, False, False)
            multiply(mid, 0, c, band, 0, False, True)
            mids[n] = mid

        def band_tiles(band):
            total = result.tile([P, PACK, BAND_ROWS, W], F32)
            shifted = work.tile([P, PACK, BAND_ROWS, W + 1], F32)
            totals[band] = total
            shifteds[band] = shifted

        def gradient(n):
            band, c = divmod(n, PACK)
            return g_sb[:, c, N_TILE * band : N_TILE * (band + 1)].rearrange("p (r j) -> p r j", j=W)

        def copy_vert(n):
            band, c = divmod(n, PACK)
            nc.scalar.copy(out=shifteds[band][:, c, :, 1 : W + 1], in_=verts[n][:])
            nc.scalar.copy(out=shifteds[band][:, c, :, 0:1], in_=verts[n][:, :, 0:1])

        def add_left(n):
            band, c = divmod(n, PACK)
            nc.gpsimd.tensor_tensor(
                out=totals[band][:, c, :, :],
                in0=totals[band][:, c, :, :],
                in1=shifteds[band][:, c, :, 0:W],
                op=ALU.add,
            )

        def start_tile(n):
            band, c = divmod(n, PACK)
            if c == 0:
                band_tiles(band)
            copy_vert(n)
            nc.vector.tensor_tensor(out=totals[band][:, c, :, :], in0=mids[n][:], in1=gradient(n), op=ALU.add)
            add_left(n)

        def add_right_edges(band, tiles):
            nc.vector.tensor_tensor(
                out=totals[band][:, 0:tiles, :, W - 1 : W],
                in0=totals[band][:, 0:tiles, :, W - 1 : W],
                in1=shifteds[band][:, 0:tiles, :, W : W + 1],
                op=ALU.add,
            )

        def add_right(n):
            band, c = divmod(n, PACK)
            nc.vector.tensor_tensor(
                out=totals[band][:, c, :, 0 : W - 1],
                in0=totals[band][:, c, :, 0 : W - 1],
                in1=verts[n][:, :, 1:W],
                op=ALU.add,
            )

        def store(n):
            band, c = divmod(n, PACK)
            nc.sync.dma_start(
                out=out_rows[:, c, N_TILE * band : N_TILE * (band + 1)],
                in_=totals[band][:, c, :, :].rearrange("p r j -> p (r j)"),
            )

        def add_mid(n):
            band, c = divmod(n, PACK)
            nc.vector.tensor_tensor(
                out=totals[band][:, c, :, :], in0=totals[band][:, c, :, :], in1=mids[n][:], op=ALU.add
            )
            store(n)

        for n in range(-LEAD, LAST_FIRST):
            ending = n - RIGHT_LAG
            ends_band = ending >= 0 and ending % PACK == PACK - 1
            if 0 <= n < LAST_FIRST:
                vert_passes(n)
                mid_passes(n)
                start_tile(n)
            if by_sign(n + LEAD + SIGN_LEAD):
                sign(n + LEAD + SIGN_LEAD)
            if by_sign(n + LEAD + 1):
                clip(n + LEAD + 1)
            if n + LEAD < PIECES:
                mask(n + LEAD)
            if 0 <= n + LEAD - QUANTISE_LAG < PIECES:
                quantise(n + LEAD - QUANTISE_LAG)
            if ends_band:
                add_right_edges(ending // PACK, PACK)
                for complete in range(ending - PACK + 1, ending):
                    store(complete)
            if 0 <= ending:
                add_right(ending)
            if ends_band:
                store(ending)

        first = LAST_FIRST
        band_tiles(LAST_BAND)

        def right_and_gradient(n):
            nc.vector.tensor_tensor(
                out=totals[LAST_BAND][:, n - first, :, 0 : W - 1],
                in0=verts[n][:, :, 1:W],
                in1=gradient(n)[:, :, 0 : W - 1],
                op=ALU.add,
            )

        def neighbours(n):
            c = n - first
            right_and_gradient(n)
            nc.vector.tensor_tensor(
                out=totals[LAST_BAND][:, c, :, W - 1 : W],
                in0=shifteds[LAST_BAND][:, c, :, W : W + 1],
                in1=gradient(n)[:, :, W - 1 : W],
                op=ALU.add,
            )
            add_left(n)

        vert_passes(first)
        copy_vert(first)
        add_right(first - 2)
        neighbours(first)
        vert_passes(first + 1)
        copy_vert(first + 1)
        add_right_edges(LAST_BAND - 1, PACK)
        for complete in range(first - PACK, first - 1):
            store(complete)
        add_right(first - 1)
        store(first - 1)
        neighbours(first + 1)
        vert_passes(first + 2)
        copy_vert(first + 2)
        neighbours(first + 2)
        vert_passes(LAST_TILE)
        last = totals[LAST_BAND][:, PACK - 1, :, :]
        last_vert = verts[LAST_TILE]
        for n in range(first, TILES):
            mid_passes(n)
        right_and_gradient(LAST_TILE)
        nc.vector.tensor_tensor(
            out=last[:, :, W - 1 : W],
            in0=last_vert[:, :, W - 1 : W],
            in1=gradient(LAST_TILE)[:, :, W - 1 : W],
            op=ALU.add,
        )
        add_mid(first)
        nc.vector.tensor_tensor(out=last[:, :, 1:W], in0=last[:, :, 1:W], in1=last_vert[:, :, 0 : W - 1], op=ALU.add)
        add_mid(first + 1)
        nc.vector.tensor_tensor(out=last[:, :, 0:1], in0=last[:, :, 0:1], in1=last_vert[:, :, 0:1], op=ALU.add)
        add_mid(first + 2)
        add_mid(LAST_TILE)
